import numpy as np
import ml_dtypes


def mxq(x, axis, fmt="e4m3"):
    dtype, down = {"e4m3": (ml_dtypes.float8_e4m3fn, 7), "e5m2": (ml_dtypes.float8_e5m2, 14)}[fmt]
    v = np.moveaxis(np.asarray(x, np.float32).astype(ml_dtypes.bfloat16).astype(np.float64), axis, -1)
    blocks = v.reshape(v.shape[:-1] + (-1, 32))
    amax = np.abs(blocks).max(-1, keepdims=True)
    byte = np.maximum(np.where(amax > 0, np.frexp(amax)[1] - 1 + 127, 0) - down, 1)
    scale = np.exp2(byte - 127.0)
    codes = (blocks / scale).astype(np.float32).astype(dtype).astype(np.float64)
    return np.moveaxis((codes * scale).reshape(v.shape), -1, axis)


WIDE = False


def mx_kscale(k):
    if not WIDE:
        return np.ones(k)
    levels = np.array([10, -10, 5, -5, 0])
    a = np.random.permutation(np.resize(levels, k // 512 * 4)).reshape(k // 512, 4)
    idx = np.arange(k)
    return np.exp2(a[idx // 512, idx % 128 // 32])


BF16 = ml_dtypes.bfloat16


def bf(x):
    return np.asarray(x, np.float32).astype(BF16)


def f64(x):
    return np.asarray(x).astype(np.float64)


E2M1 = np.array([0.0, 0.5, 1.0, 1.5, 2.0, 3.0, 4.0, 6.0, -0.0, -0.5, -1.0, -1.5, -2.0, -3.0, -4.0, -6.0])


def pack_weight(w, fmt):
    k, n = w.shape
    w = f64(bf(w)).reshape(k // 32, 32, n)
    amax = np.abs(w).max(1)
    if fmt == "e4m3":
        byte = np.frexp(amax)[1] - 1 + 127 - 7
    else:
        mant, ex = np.frexp(amax / 6.0)
        byte = np.where(mant > 0.5, ex, ex - 1) + 127
    byte = np.clip(np.where(amax > 0, byte, 1), 1, 254)
    scaled = (w * np.exp2(127.0 - byte)[:, None, :]).reshape(k, n).astype(np.float32)
    by_word = np.ascontiguousarray(scaled.reshape(k // 512, 128, 4, n).transpose(0, 1, 3, 2))
    if fmt == "e4m3":
        words = by_word.astype(ml_dtypes.float8_e4m3fn).view(np.uint8)
    else:
        c = by_word.astype(ml_dtypes.float4_e2m1fn).view(np.uint8) & 0xF
        words = c[..., 0::2] | (c[..., 1::2] << 4)
    return np.ascontiguousarray(words), np.ascontiguousarray(byte.astype(np.uint8).reshape(k // 512, 16, n))


def unpack_weight(words, scales, fmt):
    g, p, n, _ = words.shape
    if fmt == "e4m3":
        vals = np.ascontiguousarray(words).view(ml_dtypes.float8_e4m3fn).astype(np.float64)
    else:
        nib = np.empty((g, p, n, 4), np.uint8)
        nib[..., 0::2] = words & 0xF
        nib[..., 1::2] = words >> 4
        vals = E2M1[nib]
    vals = vals * np.repeat(np.exp2(scales.astype(np.float64) - 127.0), 8, axis=1)[..., None]
    return vals.transpose(0, 1, 3, 2).reshape(g * 512, n)


N, K, H = 1024, 1024, 128
G = 4 * H
FMT = "e4m3"


def sigmoid(v):
    return 1.0 / (1.0 + np.exp(-v))


def used(a):
    return np.concatenate([a[:H], a[2 * H:]], axis=0)


def cell(xq, w_ih_words, w_ih_scales, b_ih, b_hh):
    w_ih = unpack_weight(w_ih_words, w_ih_scales, FMT).T
    gates = (xq @ used(w_ih).T) + used(f64(b_ih)) + used(f64(b_hh))
    i, g, o = np.split(gates, 3, axis=-1)
    i = sigmoid(i)
    g = np.tanh(g)
    o = sigmoid(o)
    c = i * g
    return o * np.tanh(c)


def setup_inputs():
    s = mx_kscale(K)
    V_cells = bf(np.random.standard_normal((N, K)) * s)
    w_ih_f = np.random.standard_normal((G, K)) * 1.5 / np.sqrt(K) / s[None, :]
    w_ih_f_words, w_ih_f_scales = pack_weight(np.ascontiguousarray(w_ih_f.T), FMT)
    w_hh_f = bf(np.random.standard_normal((G, H)) / np.sqrt(H))
    b_ih_f = bf(np.random.standard_normal(G) * 0.3)
    b_hh_f = bf(np.random.standard_normal(G) * 0.3)
    w_ih_b = np.random.standard_normal((G, K)) * 1.5 / np.sqrt(K) / s[None, :]
    w_ih_b_words, w_ih_b_scales = pack_weight(np.ascontiguousarray(w_ih_b.T), FMT)
    w_hh_b = bf(np.random.standard_normal((G, H)) / np.sqrt(H))
    b_ih_b = bf(np.random.standard_normal(G) * 0.3)
    b_hh_b = bf(np.random.standard_normal(G) * 0.3)
    return {
        "V_cells": V_cells,
        "w_ih_f_words": w_ih_f_words,
        "w_ih_f_scales": w_ih_f_scales,
        "w_hh_f": w_hh_f,
        "b_ih_f": b_ih_f,
        "b_hh_f": b_hh_f,
        "w_ih_b_words": w_ih_b_words,
        "w_ih_b_scales": w_ih_b_scales,
        "w_hh_b": w_hh_b,
        "b_ih_b": b_ih_b,
        "b_hh_b": b_hh_b,
    }


def reference(V_cells, w_ih_f_words, w_ih_f_scales, w_hh_f, b_ih_f, b_hh_f, w_ih_b_words, w_ih_b_scales, w_hh_b, b_ih_b, b_hh_b):
    xq = mxq(f64(V_cells), 1, "e4m3")
    h_f = cell(xq, w_ih_f_words, w_ih_f_scales, b_ih_f, b_hh_f)
    h_b = cell(xq, w_ih_b_words, w_ih_b_scales, b_ih_b, b_hh_b)
    return np.concatenate([h_f, h_b], axis=-1)

@@ -1,0 +1,217 @@
+from contextlib import ExitStack
+
+import concourse.mybir as mybir
+from concourse.masks import make_identity
+
+F32 = mybir.dt.float32
+BF16 = mybir.dt.bfloat16
+I32 = mybir.dt.int32
+U32 = mybir.dt.uint32
+U8 = mybir.dt.uint8
+FP8X4 = mybir.dt.float8_e4m3fn_x4
+ACT = mybir.ActivationFunctionType
+
+P = 128
+ROWS = 1024
+K = 1024
+H = 128
+PASSES = K // (4 * P)
+ROW_TILES = ROWS // P
+CHUNK_TILES = 2
+CHUNK = CHUNK_TILES * P
+CHUNKS = ROW_TILES // CHUNK_TILES
+GATE_I, GATE_G, GATE_O = 0, 2, 3
+
+FLOPS = 2 * ROWS * K * 2 * 3 * H
+BYTES = ROWS * K * 2 + 2 * (K * 3 * H + (K // 32) * 3 * H + 2 * 3 * H * 2) + ROWS * 2 * H * 4
+
+
+def tile_predictionbilstm_kernel(
+    tc,
+    V_cells,
+    w_ih_f_words,
+    w_ih_f_scales,
+    w_hh_f,
+    b_ih_f,
+    b_hh_f,
+    w_ih_b_words,
+    w_ih_b_scales,
+    w_hh_b,
+    b_ih_b,
+    b_hh_b,
+    out,
+):
+    nc = tc.nc
+    x_rows = V_cells.rearrange("(p t) k -> p t k", t=ROW_TILES)
+    out_rows = out.rearrange("(p t) c -> p t c", t=ROW_TILES)
+
+    with ExitStack() as ctx:
+        keep = ctx.enter_context(tc.tile_pool(name="keep", bufs=1))
+        quant = ctx.enter_context(tc.tile_pool(name="quant", bufs=CHUNKS))
+        work = ctx.enter_context(tc.tile_pool(name="work", bufs=3))
+        flip_ps = ctx.enter_context(tc.psum_pool(name="flip_ps", bufs=3))
+        gate_ps = ctx.enter_context(tc.psum_pool(name="gate_ps", bufs=5))
+        ctx.enter_context(tc.manual_schedule())
+
+        x_sb = keep.tile([P, ROW_TILES, K], BF16)
+        w_codes = keep.tile([P, 2, PASSES, 4 * H], U32, align_bytes=64)
+        w_scales = keep.tile([P, 2, PASSES, 4 * H], U8, align_bytes=64)
+        bias_rows = keep.tile([P, H], BF16)
+        ident = keep.tile([P, P], F32)
+        pick = keep.tile([P, 32], BF16)
+        bias_cols = keep.tile([P, 32], F32)
+        warm = keep.tile([P, 1], F32)
+
+        def load_x(c):
+            tiles = slice(c * CHUNK_TILES, (c + 1) * CHUNK_TILES)
+            nc.sync.dma_start(out=x_sb[:, tiles, :], in_=x_rows[:, tiles, :])
+
+        def load_w_codes(d, words):
+            nc.sync.dma_start(
+                out=w_codes[:, d, :, :].bitcast(I32),
+                in_=words.rearrange("g p n t -> p g (n t)").bitcast(I32),
+            )
+
+        def load_w_scales(d, scales, queue, view):
+            for quad in range(4):
+                queue.dma_start(
+                    out=w_scales[32 * quad : 32 * quad + 4, d, :, :].bitcast(view),
+                    in_=scales[:, 4 * quad : 4 * quad + 4, :].rearrange("g r n -> r g n").bitcast(view),
+                )
+
+        nc.vector.memset(bias_rows[:], 0.0)
+        nc.vector.memset(w_scales[:].rearrange("p d g n -> p (d g n)").bitcast(I32), 0)
+        nc.vector.memset(warm[:], 0.0)
+        make_identity(nc, ident[:])
+
+        load_x(0)
+        for row, vec in ((0, b_ih_f), (4, b_ih_b), (8, b_hh_f), (12, b_hh_b)):
+            nc.scalar.dma_start(out=bias_rows[row : row + 4, :], in_=vec.rearrange("(b u) -> b u", u=H))
+        nc.scalar.activation(out=warm[:], in_=warm[:], func=ACT.Sigmoid)
+        load_x(1)
+        load_w_codes(0, w_ih_f_words)
+        load_w_scales(0, w_ih_f_scales, nc.sync, I32)
+        load_w_codes(1, w_ih_b_words)
+        load_x(2)
+        load_x(3)
+        load_w_scales(1, w_ih_b_scales, nc.gpsimd, F32)
+
+        def make_bias_cols():
+            bias_ps = flip_ps.tile([P, 32], F32, tag="flip")
+            nc.tensor.matmul(out=bias_ps[:], lhsT=bias_rows[:], rhs=pick[:], start=True, stop=True)
+            nc.vector.tensor_copy(out=bias_cols[:], in_=bias_ps[:])
+
+        def bias_of(d, block):
+            return bias_cols[:, 4 * d + block : 4 * d + block + 1]
+
+        grouped = {}
+        x_codes = {}
+        x_scales = {}
+        acc_ig = {}
+        acc_o = {}
+        sig_i, tanh_g, sig_o, cell, hidden = {}, {}, {}, {}, {}
+
+        def flip_in(c, odd_copy):
+            grouped[c] = quant.tile([P, PASSES, CHUNK, 4], BF16, align_bytes=64, name="grouped")
+            grouped_words = (
+                grouped[c][:]
+                .rearrange("p g m t -> p (g m t)")
+                .bitcast(F32)
+                .rearrange("p (g m u) -> p g m u", g=PASSES, u=2)
+            )
+            for j in range(CHUNK_TILES):
+                x_words = x_sb[:, c * CHUNK_TILES + j, :].bitcast(F32)
+                flipped = flip_ps.tile([P, PASSES, 2, P], F32, tag="flip")
+                for g in range(PASSES):
+                    for u in range(2):
+                        nc.tensor.transpose(
+                            flipped[:, g, u, :], x_words[:, 256 * g + u : 256 * (g + 1) : 2], ident[:]
+                        )
+                copy = nc.vector.tensor_copy if j % 2 == 0 else odd_copy
+                copy(
+                    out=grouped_words[:, :, j * P : (j + 1) * P, :],
+                    in_=flipped[:].rearrange("p g u m -> p g m u"),
+                )
+
+        def quantise(c):
+            x_codes[c] = quant.tile([P, PASSES, CHUNK], U32, align_bytes=64, name="x_codes")
+            x_scales[c] = quant.tile([P, PASSES, CHUNK], U8, align_bytes=64, name="x_scales")
+            nc.vector.quantize_mx(
+                out=x_codes[c][:].rearrange("p g m -> p (g m)").bitcast(FP8X4),
+                scales=x_scales[c][:].rearrange("p g m -> p (g m)"),
+                in_=grouped[c][:].rearrange("p g m t -> p (g m t)"),
+            )
+
+        def gate_sums(c, d, block, sums):
+            units = slice(block * H, (block + 1) * H)
+            for g in range(PASSES):
+                nc.tensor.matmul_mx(
+                    out=sums,
+                    lhsT=w_codes[:, d, g, units].bitcast(FP8X4),
+                    lhsT_scale=w_scales[:, d, g, units],
+                    rhs=x_codes[c][:, g, :].bitcast(FP8X4),
+                    rhs_scale=x_scales[c][:, g, :],
+                    start=(g == 0),
+                    stop=(g == PASSES - 1),
+                )
+
+        def multiply(c):
+            for d in range(2):
+                acc_ig[c, d] = gate_ps.tile([P, 2, CHUNK], F32, name="acc")
+                gate_sums(c, d, GATE_I, acc_ig[c, d][:, 0, :])
+                gate_sums(c, d, GATE_G, acc_ig[c, d][:, 1, :])
+            acc_o[c] = gate_ps.tile([P, 2, CHUNK], F32, name="acc")
+            for d in range(2):
+                gate_sums(c, d, GATE_O, acc_o[c][:, d, :])
+
+        def cell_state(c):
+            sig_i[c] = work.tile([P, 2, CHUNK], F32, name="sig_i")
+            tanh_g[c] = work.tile([P, 2, CHUNK], F32, name="tanh_g")
+            cell[c] = work.tile([P, 2, CHUNK], F32, name="cell")
+            for d in range(2):
+                nc.scalar.activation(
+                    out=sig_i[c][:, d, :], in_=acc_ig[c, d][:, 0, :], func=ACT.Sigmoid, bias=bias_of(d, GATE_I)
+                )
+                nc.scalar.activation(
+                    out=tanh_g[c][:, d, :], in_=acc_ig[c, d][:, 1, :], func=ACT.Tanh, bias=bias_of(d, GATE_G)
+                )
+                nc.vector.tensor_mul(out=cell[c][:, d, :], in0=sig_i[c][:, d, :], in1=tanh_g[c][:, d, :])
+
+        def hidden_state(c):
+            sig_o[c] = work.tile([P, 2, CHUNK], F32, name="sig_o")
+            tanh_c = work.tile([P, 2, CHUNK], F32)
+            hidden[c] = work.tile([P, 2, CHUNK], F32, name="hidden")
+            for d in range(2):
+                nc.scalar.activation(
+                    out=sig_o[c][:, d, :], in_=acc_o[c][:, d, :], func=ACT.Sigmoid, bias=bias_of(d, GATE_O)
+                )
+                nc.scalar.activation(out=tanh_c[:, d, :], in_=cell[c][:, d, :], func=ACT.Tanh)
+                nc.vector.tensor_mul(out=hidden[c][:, d, :], in0=sig_o[c][:, d, :], in1=tanh_c[:, d, :])
+
+        def flip_out(c):
+            h_rows_ps = flip_ps.tile([P, CHUNK_TILES, 2, H], F32, tag="flip")
+            for j in range(CHUNK_TILES):
+                for d in range(2):
+                    nc.tensor.transpose(h_rows_ps[:, j, d, :], hidden[c][:, d, j * P : (j + 1) * P], ident[:])
+            h_rows = work.tile([P, CHUNK_TILES, 2 * H], F32)
+            nc.vector.tensor_copy(out=h_rows[:], in_=h_rows_ps[:].rearrange("p j d u -> p j (d u)"))
+            tiles = slice(c * CHUNK_TILES, (c + 1) * CHUNK_TILES)
+            nc.sync.dma_start(out=out_rows[:, tiles, :], in_=h_rows[:])
+
+        nc.vector.tensor_add(out=pick[:], in0=ident[:, 0:32], in1=ident[:, 8:40])
+        flip_in(0, nc.scalar.copy)
+        make_bias_cols()
+        quantise(0)
+        flip_in(1, nc.scalar.copy)
+        quantise(1)
+        for c in range(CHUNKS):
+            multiply(c)
+            cell_state(c)
+            if c + 2 < CHUNKS:
+                flip_in(c + 2, nc.vector.tensor_copy)
+                quantise(c + 2)
+            if c >= 2:
+                flip_out(c - 2)
+            hidden_state(c)
+        flip_out(CHUNKS - 2)
+        flip_out(CHUNKS - 1)

@@ -72,11 +72,11 @@ def tile_predictionbilstm_kernel(
                 in_=words.rearrange("g p n t -> p g (n t)").bitcast(I32),
             )
 
-        def load_w_scales(d, scales, queue, view):
+        def load_w_scales(d, scales):
             for quad in range(4):
-                queue.dma_start(
-                    out=w_scales[32 * quad : 32 * quad + 4, d, :, :].bitcast(view),
-                    in_=scales[:, 4 * quad : 4 * quad + 4, :].rearrange("g r n -> r g n").bitcast(view),
+                nc.sync.dma_start(
+                    out=w_scales[32 * quad : 32 * quad + 4, d, :, :].bitcast(I32),
+                    in_=scales[:, 4 * quad : 4 * quad + 4, :].rearrange("g r n -> r g n").bitcast(I32),
                 )
 
         nc.vector.memset(bias_rows[:], 0.0)
@@ -90,11 +90,11 @@ def tile_predictionbilstm_kernel(
         nc.scalar.activation(out=warm[:], in_=warm[:], func=ACT.Sigmoid)
         load_x(1)
         load_w_codes(0, w_ih_f_words)
-        load_w_scales(0, w_ih_f_scales, nc.sync, I32)
+        load_w_scales(0, w_ih_f_scales)
         load_w_codes(1, w_ih_b_words)
+        load_w_scales(1, w_ih_b_scales)
         load_x(2)
         load_x(3)
-        load_w_scales(1, w_ih_b_scales, nc.gpsimd, F32)
 
         def make_bias_cols():
             bias_ps = flip_ps.tile([P, 32], F32, tag="flip")

@@ -101,6 +101,12 @@ def tile_predictionbilstm_kernel(
             nc.tensor.matmul(out=bias_ps[:], lhsT=bias_rows[:], rhs=pick[:], start=True, stop=True)
             nc.vector.tensor_copy(out=bias_cols[:], in_=bias_ps[:])
 
+        busy_ps = gate_ps.tile([P, P], F32, name="acc")
+
+        def keep_busy(times):
+            for repeat in range(times):
+                nc.tensor.matmul(out=busy_ps[:], lhsT=ident[:], rhs=ident[:], start=True, stop=True)
+
         def bias_of(d, block):
             return bias_cols[:, 4 * d + block : 4 * d + block + 1]
 
@@ -199,10 +205,13 @@ def tile_predictionbilstm_kernel(
             nc.sync.dma_start(out=out_rows[:, tiles, :], in_=h_rows[:])
 
         nc.vector.tensor_add(out=pick[:], in0=ident[:, 0:32], in1=ident[:, 8:40])
+        keep_busy(4)
         flip_in(0, nc.scalar.copy)
+        keep_busy(2)
         make_bias_cols()
         quantise(0)
         flip_in(1, nc.scalar.copy)
+        keep_busy(3)
         quantise(1)
         for c in range(CHUNKS):
             multiply(c)

@@ -44,27 +44,28 @@ def tile_predictionbilstm_kernel(
     nc = tc.nc
     x_rows = V_cells.rearrange("(p t) k -> p t k", t=ROW_TILES)
     out_rows = out.rearrange("(p t) c -> p t c", t=ROW_TILES)
+    BOTH = (0, 1)
 
     with ExitStack() as ctx:
         keep = ctx.enter_context(tc.tile_pool(name="keep", bufs=1))
         quant = ctx.enter_context(tc.tile_pool(name="quant", bufs=CHUNKS))
         work = ctx.enter_context(tc.tile_pool(name="work", bufs=3))
-        flip_ps = ctx.enter_context(tc.psum_pool(name="flip_ps", bufs=3))
-        gate_ps = ctx.enter_context(tc.psum_pool(name="gate_ps", bufs=5))
+        outbound = ctx.enter_context(tc.tile_pool(name="outbound", bufs=CHUNKS + 1))
+        banks = ctx.enter_context(tc.psum_pool(name="banks", bufs=8))
         ctx.enter_context(tc.manual_schedule())
 
         x_sb = keep.tile([P, ROW_TILES, K], BF16)
         w_codes = keep.tile([P, 2, PASSES, 4 * H], U32, align_bytes=64)
         w_scales = keep.tile([P, 2, PASSES, 4 * H], U8, align_bytes=64)
-        bias_rows = keep.tile([P, H], BF16)
+        bias_rows = keep.tile([P, 2, H], BF16)
         ident = keep.tile([P, P], F32)
         pick = keep.tile([P, 32], BF16)
-        bias_cols = keep.tile([P, 32], F32)
+        bias_cols = keep.tile([P, 2, 32], F32)
         warm = keep.tile([P, 1], F32)
+        zeros = keep.tile([P, P], F32)
 
-        def load_x(c):
-            tiles = slice(c * CHUNK_TILES, (c + 1) * CHUNK_TILES)
-            nc.sync.dma_start(out=x_sb[:, tiles, :], in_=x_rows[:, tiles, :])
+        def load_x(queue, first, count):
+            queue.dma_start(out=x_sb[:, first : first + count, :], in_=x_rows[:, first : first + count, :])
 
         def load_w_codes(d, words):
             nc.sync.dma_start(
@@ -79,43 +80,48 @@ def tile_predictionbilstm_kernel(
                     in_=scales[:, 4 * quad : 4 * quad + 4, :].rearrange("g r n -> r g n").bitcast(I32),
                 )
 
-        nc.vector.memset(bias_rows[:], 0.0)
+        def load_bias(d, b_ih, b_hh):
+            for row, vec in ((0, b_ih), (8, b_hh)):
+                nc.sync.dma_start(out=bias_rows[row : row + 4, d, :], in_=vec.rearrange("(b u) -> b u", u=H))
+
+        nc.vector.memset(zeros[:], 0.0)
         nc.vector.memset(w_scales[:].rearrange("p d g n -> p (d g n)").bitcast(I32), 0)
+        nc.vector.memset(bias_rows[:].rearrange("p d u -> p (d u)"), 0.0)
         nc.vector.memset(warm[:], 0.0)
         make_identity(nc, ident[:])
-
-        load_x(0)
-        for row, vec in ((0, b_ih_f), (4, b_ih_b), (8, b_hh_f), (12, b_hh_b)):
-            nc.scalar.dma_start(out=bias_rows[row : row + 4, :], in_=vec.rearrange("(b u) -> b u", u=H))
         nc.scalar.activation(out=warm[:], in_=warm[:], func=ACT.Sigmoid)
-        load_x(1)
+
+        load_x(nc.sync, 0, 1)
+        load_x(nc.sync, 1, 1)
         load_w_codes(0, w_ih_f_words)
         load_w_scales(0, w_ih_f_scales)
+        load_bias(0, b_ih_f, b_hh_f)
+        load_x(nc.gpsimd, 2, 2)
         load_w_codes(1, w_ih_b_words)
         load_w_scales(1, w_ih_b_scales)
-        load_x(2)
-        load_x(3)
+        load_bias(1, b_ih_b, b_hh_b)
+        load_x(nc.gpsimd, 4, 2)
+        load_x(nc.gpsimd, 6, 2)
 
-        def make_bias_cols():
-            bias_ps = flip_ps.tile([P, 32], F32, tag="flip")
-            nc.tensor.matmul(out=bias_ps[:], lhsT=bias_rows[:], rhs=pick[:], start=True, stop=True)
-            nc.vector.tensor_copy(out=bias_cols[:], in_=bias_ps[:])
+        def make_bias_cols(d):
+            bias_ps = banks.tile([P, 32], F32, tag="bank")
+            nc.tensor.matmul(out=bias_ps[:], lhsT=bias_rows[:, d, :], rhs=pick[:], start=True, stop=True)
+            nc.scalar.copy(out=bias_cols[:, d, :], in_=bias_ps[:])
 
-        busy_ps = gate_ps.tile([P, P], F32, name="acc")
+        busy_ps = banks.tile([P, P], F32, tag="bank")
 
         def keep_busy(times):
             for repeat in range(times):
-                nc.tensor.matmul(out=busy_ps[:], lhsT=ident[:], rhs=ident[:], start=True, stop=True)
+                nc.tensor.matmul(out=busy_ps[:], lhsT=zeros[:], rhs=zeros[:], start=True, stop=True)
 
         def bias_of(d, block):
-            return bias_cols[:, 4 * d + block : 4 * d + block + 1]
+            return bias_cols[:, d, block : block + 1]
 
         grouped = {}
         x_codes = {}
         x_scales = {}
-        acc_ig = {}
-        acc_o = {}
-        sig_i, tanh_g, sig_o, cell, hidden = {}, {}, {}, {}, {}
+        sums = {}
+        sig_i, tanh_g, sig_o, cell, tanh_c, hidden = {}, {}, {}, {}, {}, {}
 
         def flip_in(c, odd_copy):
             grouped[c] = quant.tile([P, PASSES, CHUNK, 4], BF16, align_bytes=64, name="grouped")
@@ -127,7 +133,7 @@ def tile_predictionbilstm_kernel(
             )
             for j in range(CHUNK_TILES):
                 x_words = x_sb[:, c * CHUNK_TILES + j, :].bitcast(F32)
-                flipped = flip_ps.tile([P, PASSES, 2, P], F32, tag="flip")
+                flipped = banks.tile([P, PASSES, 2, P], F32, tag="bank")
                 for g in range(PASSES):
                     for u in range(2):
                         nc.tensor.transpose(
@@ -148,11 +154,12 @@ def tile_predictionbilstm_kernel(
                 in_=grouped[c][:].rearrange("p g m t -> p (g m t)"),
             )
 
-        def gate_sums(c, d, block, sums):
+        def gate_sums(c, d, block, acc):
+            sums[c, d, block] = acc
             units = slice(block * H, (block + 1) * H)
             for g in range(PASSES):
                 nc.tensor.matmul_mx(
-                    out=sums,
+                    out=acc,
                     lhsT=w_codes[:, d, g, units].bitcast(FP8X4),
                     lhsT_scale=w_scales[:, d, g, units],
                     rhs=x_codes[c][:, g, :].bitcast(FP8X4),
@@ -161,66 +168,111 @@ def tile_predictionbilstm_kernel(
                     stop=(g == PASSES - 1),
                 )
 
-        def multiply(c):
-            for d in range(2):
-                acc_ig[c, d] = gate_ps.tile([P, 2, CHUNK], F32, name="acc")
-                gate_sums(c, d, GATE_I, acc_ig[c, d][:, 0, :])
-                gate_sums(c, d, GATE_G, acc_ig[c, d][:, 1, :])
-            acc_o[c] = gate_ps.tile([P, 2, CHUNK], F32, name="acc")
-            for d in range(2):
-                gate_sums(c, d, GATE_O, acc_o[c][:, d, :])
+        def multiply_in(c, d):
+            acc = banks.tile([P, 2, CHUNK], F32, tag="bank")
+            gate_sums(c, d, GATE_I, acc[:, 0, :])
+            gate_sums(c, d, GATE_G, acc[:, 1, :])
 
-        def cell_state(c):
-            sig_i[c] = work.tile([P, 2, CHUNK], F32, name="sig_i")
-            tanh_g[c] = work.tile([P, 2, CHUNK], F32, name="tanh_g")
-            cell[c] = work.tile([P, 2, CHUNK], F32, name="cell")
-            for d in range(2):
-                nc.scalar.activation(
-                    out=sig_i[c][:, d, :], in_=acc_ig[c, d][:, 0, :], func=ACT.Sigmoid, bias=bias_of(d, GATE_I)
-                )
-                nc.scalar.activation(
-                    out=tanh_g[c][:, d, :], in_=acc_ig[c, d][:, 1, :], func=ACT.Tanh, bias=bias_of(d, GATE_G)
-                )
-                nc.vector.tensor_mul(out=cell[c][:, d, :], in0=sig_i[c][:, d, :], in1=tanh_g[c][:, d, :])
+        def multiply_out(c, dirs):
+            acc = banks.tile([P, len(dirs), CHUNK], F32, tag="bank")
+            for s, d in enumerate(dirs):
+                gate_sums(c, d, GATE_O, acc[:, s, :])
 
-        def hidden_state(c):
-            sig_o[c] = work.tile([P, 2, CHUNK], F32, name="sig_o")
-            tanh_c = work.tile([P, 2, CHUNK], F32)
-            hidden[c] = work.tile([P, 2, CHUNK], F32, name="hidden")
-            for d in range(2):
-                nc.scalar.activation(
-                    out=sig_o[c][:, d, :], in_=acc_o[c][:, d, :], func=ACT.Sigmoid, bias=bias_of(d, GATE_O)
-                )
-                nc.scalar.activation(out=tanh_c[:, d, :], in_=cell[c][:, d, :], func=ACT.Tanh)
-                nc.vector.tensor_mul(out=hidden[c][:, d, :], in0=sig_o[c][:, d, :], in1=tanh_c[:, d, :])
+        def new_chunk(c):
+            for store, name in ((sig_i, "sig_i"), (tanh_g, "tanh_g"), (sig_o, "sig_o"), (cell, "cell"),
+                                (tanh_c, "tanh_c"), (hidden, "hidden")):
+                store[c] = work.tile([P, 2, CHUNK], F32, name=name)
 
-        def flip_out(c):
-            h_rows_ps = flip_ps.tile([P, CHUNK_TILES, 2, H], F32, tag="flip")
+        def part(tile_, dirs):
+            return tile_[:, dirs[0] : dirs[-1] + 1, :]
+
+        def squash_in(c, d):
+            nc.scalar.activation(out=sig_i[c][:, d, :], in_=sums[c, d, GATE_I], func=ACT.Sigmoid, bias=bias_of(d, GATE_I))
+            nc.scalar.activation(out=tanh_g[c][:, d, :], in_=sums[c, d, GATE_G], func=ACT.Tanh, bias=bias_of(d, GATE_G))
+
+        def squash_out(c, d):
+            nc.scalar.activation(out=sig_o[c][:, d, :], in_=sums[c, d, GATE_O], func=ACT.Sigmoid, bias=bias_of(d, GATE_O))
+
+        def cell_state(c, dirs):
+            nc.vector.tensor_mul(out=part(cell[c], dirs), in0=part(sig_i[c], dirs), in1=part(tanh_g[c], dirs))
+
+        def squash_cell(c, dirs):
+            nc.scalar.activation(out=part(tanh_c[c], dirs), in_=part(cell[c], dirs), func=ACT.Tanh)
+
+        def hidden_state(engine, c, dirs):
+            engine.tensor_mul(out=part(hidden[c], dirs), in0=part(sig_o[c], dirs), in1=part(tanh_c[c], dirs))
+
+        flipped_back = {}
+
+        def flip_out(c, dirs):
+            flipped_back[c, dirs] = banks.tile([P, CHUNK_TILES, len(dirs), H], F32, tag="bank", name="flipped_back")
             for j in range(CHUNK_TILES):
-                for d in range(2):
-                    nc.tensor.transpose(h_rows_ps[:, j, d, :], hidden[c][:, d, j * P : (j + 1) * P], ident[:])
-            h_rows = work.tile([P, CHUNK_TILES, 2 * H], F32)
-            nc.vector.tensor_copy(out=h_rows[:], in_=h_rows_ps[:].rearrange("p j d u -> p j (d u)"))
+                for s, d in enumerate(dirs):
+                    nc.tensor.transpose(flipped_back[c, dirs][:, j, s, :], hidden[c][:, d, j * P : (j + 1) * P], ident[:])
+
+        def store(c, dirs):
+            h_rows = outbound.tile([P, CHUNK_TILES, len(dirs) * H], F32, name="h_rows")
+            nc.vector.tensor_copy(out=h_rows[:], in_=flipped_back[c, dirs][:].rearrange("p j d u -> p j (d u)"))
             tiles = slice(c * CHUNK_TILES, (c + 1) * CHUNK_TILES)
-            nc.sync.dma_start(out=out_rows[:, tiles, :], in_=h_rows[:])
+            nc.sync.dma_start(out=out_rows[:, tiles, dirs[0] * H : (dirs[-1] + 1) * H], in_=h_rows[:])
 
         nc.vector.tensor_add(out=pick[:], in0=ident[:, 0:32], in1=ident[:, 8:40])
-        keep_busy(4)
-        flip_in(0, nc.scalar.copy)
-        keep_busy(2)
-        make_bias_cols()
-        quantise(0)
-        flip_in(1, nc.scalar.copy)
+        new_chunk(0)
         keep_busy(3)
+        flip_in(0, nc.scalar.copy)
+        quantise(0)
+        keep_busy(3)
+        make_bias_cols(0)
+        multiply_in(0, 0)
+        squash_in(0, 0)
+        flip_in(1, nc.scalar.copy)
+        cell_state(0, (0,))
         quantise(1)
-        for c in range(CHUNKS):
-            multiply(c)
-            cell_state(c)
-            if c + 2 < CHUNKS:
-                flip_in(c + 2, nc.vector.tensor_copy)
-                quantise(c + 2)
-            if c >= 2:
-                flip_out(c - 2)
-            hidden_state(c)
-        flip_out(CHUNKS - 2)
-        flip_out(CHUNKS - 1)
+        multiply_out(0, (0,))
+        squash_out(0, 0)
+        multiply_in(0, 1)
+        make_bias_cols(1)
+        multiply_out(0, (1,))
+        squash_in(0, 1)
+        squash_cell(0, (0,))
+        hidden_state(nc.gpsimd, 0, (0,))
+        cell_state(0, (1,))
+        squash_out(0, 1)
+        squash_cell(0, (1,))
+        hidden_state(nc.gpsimd, 0, (1,))
+        for c in (1, 2):
+            new_chunk(c)
+            flip_in(c + 1, nc.vector.tensor_copy)
+            quantise(c + 1)
+            for d in BOTH:
+                multiply_in(c, d)
+            multiply_out(c, BOTH)
+            for d in BOTH:
+                squash_in(c, d)
+            for d in BOTH:
+                squash_out(c, d)
+            cell_state(c, BOTH)
+            squash_cell(c, BOTH)
+            hidden_state(nc.gpsimd, c, BOTH)
+        flip_out(0, BOTH)
+        store(0, BOTH)
+        new_chunk(3)
+        for d in BOTH:
+            multiply_in(3, d)
+        for d in BOTH:
+            multiply_out(3, (d,))
+        flip_out(1, BOTH)
+        for d in BOTH:
+            squash_in(3, d)
+            cell_state(3, (d,))
+        store(1, BOTH)
+        for d in BOTH:
+            squash_out(3, d)
+            squash_cell(3, (d,))
+            hidden_state(nc.vector, 3, (d,))
+        flip_out(2, BOTH)
+        store(2, BOTH)
+        for d in BOTH:
+            flip_out(3, (d,))
+        for d in BOTH:
+            store(3, (d,))

@@ -235,15 +235,14 @@ def tile_predictionbilstm_kernel(
         multiply_out(0, (1,))
         squash_in(0, 1)
         squash_cell(0, (0,))
-        hidden_state(nc.gpsimd, 0, (0,))
         cell_state(0, (1,))
         squash_out(0, 1)
         squash_cell(0, (1,))
-        hidden_state(nc.gpsimd, 0, (1,))
         for c in (1, 2):
             new_chunk(c)
             flip_in(c + 1, nc.vector.tensor_copy)
             quantise(c + 1)
+            hidden_state(nc.vector, c - 1, BOTH)
             for d in BOTH:
                 multiply_in(c, d)
             multiply_out(c, BOTH)
@@ -253,9 +252,9 @@ def tile_predictionbilstm_kernel(
                 squash_out(c, d)
             cell_state(c, BOTH)
             squash_cell(c, BOTH)
-            hidden_state(nc.gpsimd, c, BOTH)
         flip_out(0, BOTH)
         store(0, BOTH)
+        hidden_state(nc.vector, 2, BOTH)
         new_chunk(3)
         for d in BOTH:
             multiply_in(3, d)

@@ -93,15 +93,15 @@ def tile_predictionbilstm_kernel(
 
         load_x(nc.sync, 0, 1)
         load_x(nc.sync, 1, 1)
-        load_w_codes(0, w_ih_f_words)
         load_w_scales(0, w_ih_f_scales)
+        load_w_codes(0, w_ih_f_words)
+        load_x(nc.sync, 2, 2)
         load_bias(0, b_ih_f, b_hh_f)
-        load_x(nc.gpsimd, 2, 2)
         load_w_codes(1, w_ih_b_words)
         load_w_scales(1, w_ih_b_scales)
+        load_x(nc.sync, 4, 2)
         load_bias(1, b_ih_b, b_hh_b)
-        load_x(nc.gpsimd, 4, 2)
-        load_x(nc.gpsimd, 6, 2)
+        load_x(nc.sync, 6, 2)
 
         def make_bias_cols(d):
             bias_ps = banks.tile([P, 32], F32, tag="bank")

@@ -94,12 +94,12 @@ def tile_predictionbilstm_kernel(
         load_x(nc.sync, 0, 1)
         load_x(nc.sync, 1, 1)
         load_w_scales(0, w_ih_f_scales)
-        load_w_codes(0, w_ih_f_words)
         load_x(nc.sync, 2, 2)
+        load_w_codes(0, w_ih_f_words)
         load_bias(0, b_ih_f, b_hh_f)
+        load_x(nc.sync, 4, 2)
         load_w_codes(1, w_ih_b_words)
         load_w_scales(1, w_ih_b_scales)
-        load_x(nc.sync, 4, 2)
         load_bias(1, b_ih_b, b_hh_b)
         load_x(nc.sync, 6, 2)
 
@@ -210,50 +210,69 @@ def tile_predictionbilstm_kernel(
                 for s, d in enumerate(dirs):
                     nc.tensor.transpose(flipped_back[c, dirs][:, j, s, :], hidden[c][:, d, j * P : (j + 1) * P], ident[:])
 
-        def store(c, dirs):
+        def store(copy, c, dirs):
             h_rows = outbound.tile([P, CHUNK_TILES, len(dirs) * H], F32, name="h_rows")
-            nc.vector.tensor_copy(out=h_rows[:], in_=flipped_back[c, dirs][:].rearrange("p j d u -> p j (d u)"))
+            copy(out=h_rows[:], in_=flipped_back[c, dirs][:].rearrange("p j d u -> p j (d u)"))
             tiles = slice(c * CHUNK_TILES, (c + 1) * CHUNK_TILES)
             nc.sync.dma_start(out=out_rows[:, tiles, dirs[0] * H : (dirs[-1] + 1) * H], in_=h_rows[:])
 
         nc.vector.tensor_add(out=pick[:], in0=ident[:, 0:32], in1=ident[:, 8:40])
+        FWD, BWD = 0, 1
+        by_vector, by_scalar = nc.vector.tensor_copy, nc.scalar.copy
+
+        def multiply(c, d):
+            multiply_in(c, d)
+            multiply_out(c, (d,))
+
         new_chunk(0)
+        new_chunk(1)
         keep_busy(3)
-        flip_in(0, nc.scalar.copy)
-        quantise(0)
-        keep_busy(3)
-        make_bias_cols(0)
-        multiply_in(0, 0)
-        squash_in(0, 0)
-        flip_in(1, nc.scalar.copy)
-        cell_state(0, (0,))
-        quantise(1)
-        multiply_out(0, (0,))
-        squash_out(0, 0)
-        multiply_in(0, 1)
-        make_bias_cols(1)
-        multiply_out(0, (1,))
-        squash_in(0, 1)
-        squash_cell(0, (0,))
-        cell_state(0, (1,))
-        squash_out(0, 1)
-        squash_cell(0, (1,))
-        for c in (1, 2):
-            new_chunk(c)
-            flip_in(c + 1, nc.vector.tensor_copy)
-            quantise(c + 1)
-            hidden_state(nc.vector, c - 1, BOTH)
-            for d in BOTH:
-                multiply_in(c, d)
-            multiply_out(c, BOTH)
-            for d in BOTH:
-                squash_in(c, d)
-            for d in BOTH:
-                squash_out(c, d)
-            cell_state(c, BOTH)
-            squash_cell(c, BOTH)
+        for c in (0, 1):
+            flip_in(c, by_scalar)
+            quantise(c)
+        make_bias_cols(FWD)
+        multiply(0, FWD)
+        squash_in(0, FWD)
+        squash_out(0, FWD)
+        cell_state(0, (FWD,))
+        flip_in(2, by_scalar)
+        squash_cell(0, (FWD,))
+        multiply(1, FWD)
+        squash_in(1, FWD)
+        squash_out(1, FWD)
+        cell_state(1, (FWD,))
+        hidden_state(nc.vector, 0, (FWD,))
+        quantise(2)
+        multiply_in(0, BWD)
+        make_bias_cols(BWD)
+        multiply_out(0, (BWD,))
+        squash_cell(1, (FWD,))
+        hidden_state(nc.vector, 1, (FWD,))
+        multiply(1, BWD)
+        squash_in(0, BWD)
+        cell_state(0, (BWD,))
+        squash_in(1, BWD)
+        flip_in(3, by_vector)
+        squash_out(0, BWD)
+        squash_cell(0, (BWD,))
+        hidden_state(nc.vector, 0, (BWD,))
+        cell_state(1, (BWD,))
+        quantise(3)
+        new_chunk(2)
+        for d in BOTH:
+            multiply_in(2, d)
+        multiply_out(2, BOTH)
+        for d in BOTH:
+            squash_in(2, d)
+        squash_out(1, BWD)
+        squash_cell(1, (BWD,))
+        cell_state(2, BOTH)
+        for d in BOTH:
+            squash_out(2, d)
+        squash_cell(2, BOTH)
         flip_out(0, BOTH)
-        store(0, BOTH)
+        store(by_vector, 0, BOTH)
+        hidden_state(nc.vector, 1, (BWD,))
         hidden_state(nc.vector, 2, BOTH)
         new_chunk(3)
         for d in BOTH:
@@ -261,17 +280,17 @@ def tile_predictionbilstm_kernel(
         for d in BOTH:
             multiply_out(3, (d,))
         flip_out(1, BOTH)
+        flip_out(2, BOTH)
         for d in BOTH:
             squash_in(3, d)
             cell_state(3, (d,))
-        store(1, BOTH)
+        store(by_vector, 1, BOTH)
         for d in BOTH:
             squash_out(3, d)
             squash_cell(3, (d,))
             hidden_state(nc.vector, 3, (d,))
-        flip_out(2, BOTH)
-        store(2, BOTH)
+        store(by_scalar, 2, BOTH)
         for d in BOTH:
             flip_out(3, (d,))
-        for d in BOTH:
-            store(3, (d,))
+        store(by_vector, 3, (FWD,))
+        store(by_scalar, 3, (BWD,))

@@ -235,7 +235,7 @@ def tile_predictionbilstm_kernel(
         squash_in(0, FWD)
         squash_out(0, FWD)
         cell_state(0, (FWD,))
-        flip_in(2, by_scalar)
+        flip_in(2, by_vector)
         squash_cell(0, (FWD,))
         multiply(1, FWD)
         squash_in(1, FWD)

@@ -226,10 +226,12 @@ def tile_predictionbilstm_kernel(
 
         new_chunk(0)
         new_chunk(1)
-        keep_busy(3)
-        for c in (0, 1):
-            flip_in(c, by_scalar)
-            quantise(c)
+        keep_busy(4)
+        flip_in(0, by_scalar)
+        quantise(0)
+        keep_busy(2)
+        flip_in(1, by_scalar)
+        quantise(1)
         make_bias_cols(FWD)
         multiply(0, FWD)
         squash_in(0, FWD)

@@ -181,7 +181,8 @@ def tile_predictionbilstm_kernel(
         def new_chunk(c):
             for store, name in ((sig_i, "sig_i"), (tanh_g, "tanh_g"), (sig_o, "sig_o"), (cell, "cell"),
                                 (tanh_c, "tanh_c"), (hidden, "hidden")):
-                store[c] = work.tile([P, 2, CHUNK], F32, name=name)
+                if c < CHUNKS - 1 or name != "hidden":
+                    store[c] = work.tile([P, 2, CHUNK], F32, name=name)
 
         def part(tile_, dirs):
             return tile_[:, dirs[0] : dirs[-1] + 1, :]
@@ -215,6 +216,25 @@ def tile_predictionbilstm_kernel(
             copy(out=h_rows[:], in_=flipped_back[c, dirs][:].rearrange("p j d u -> p j (d u)"))
             tiles = slice(c * CHUNK_TILES, (c + 1) * CHUNK_TILES)
             nc.sync.dma_start(out=out_rows[:, tiles, dirs[0] * H : (dirs[-1] + 1) * H], in_=h_rows[:])
+
+        gate_rows, cell_rows_ps = {}, {}
+
+        def flip_part(source, c, d):
+            flipped_part = banks.tile([P, CHUNK_TILES, H], F32, tag="bank")
+            for j in range(CHUNK_TILES):
+                nc.tensor.transpose(flipped_part[:, j, :], source[c][:, d, j * P : (j + 1) * P], ident[:])
+            return flipped_part
+
+        def flip_gate(c, d):
+            gate_ps = flip_part(sig_o, c, d)
+            gate_rows[c, d] = outbound.tile([P, CHUNK_TILES, H], F32, name="gate_rows")
+            nc.vector.tensor_copy(out=gate_rows[c, d][:], in_=gate_ps[:])
+
+        def finish(c, d):
+            h_rows = outbound.tile([P, CHUNK_TILES, H], F32, name="h_rows")
+            nc.vector.tensor_mul(out=h_rows[:], in0=cell_rows_ps[c, d][:], in1=gate_rows[c, d][:])
+            tiles = slice(c * CHUNK_TILES, (c + 1) * CHUNK_TILES)
+            nc.sync.dma_start(out=out_rows[:, tiles, d * H : (d + 1) * H], in_=h_rows[:])
 
         nc.vector.tensor_add(out=pick[:], in0=ident[:, 0:32], in1=ident[:, 8:40])
         FWD, BWD = 0, 1
@@ -289,10 +309,12 @@ def tile_predictionbilstm_kernel(
         store(by_vector, 1, BOTH)
         for d in BOTH:
             squash_out(3, d)
+        for d in BOTH:
+            flip_gate(3, d)
+        for d in BOTH:
             squash_cell(3, (d,))
-            hidden_state(nc.vector, 3, (d,))
         store(by_scalar, 2, BOTH)
         for d in BOTH:
-            flip_out(3, (d,))
-        store(by_vector, 3, (FWD,))
-        store(by_scalar, 3, (BWD,))
+            cell_rows_ps[3, d] = flip_part(tanh_c, 3, d)
+        for d in BOTH:
+            finish(3, d)

@@ -62,26 +62,28 @@ def tile_predictionbilstm_kernel(
         pick = keep.tile([P, 32], BF16)
         bias_cols = keep.tile([P, 2, 32], F32)
         warm = keep.tile([P, 1], F32)
-        zeros = keep.tile([P, P], F32)
+        zeros = keep.tile([P, P], BF16)
 
-        def load_x(queue, first, count):
-            queue.dma_start(out=x_sb[:, first : first + count, :], in_=x_rows[:, first : first + count, :])
+        def load_x(first, count):
+            nc.sync.dma_start(out=x_sb[:, first : first + count, :], in_=x_rows[:, first : first + count, :])
 
-        def load_w_codes(d, words):
+        def load_w_codes(d):
+            words = (w_ih_f_words, w_ih_b_words)[d]
             nc.sync.dma_start(
                 out=w_codes[:, d, :, :].bitcast(I32),
                 in_=words.rearrange("g p n t -> p g (n t)").bitcast(I32),
             )
 
-        def load_w_scales(d, scales):
-            for quad in range(4):
+        def load_w_scales(d, quads):
+            scales = (w_ih_f_scales, w_ih_b_scales)[d]
+            for quad in quads:
                 nc.sync.dma_start(
                     out=w_scales[32 * quad : 32 * quad + 4, d, :, :].bitcast(I32),
                     in_=scales[:, 4 * quad : 4 * quad + 4, :].rearrange("g r n -> r g n").bitcast(I32),
                 )
 
-        def load_bias(d, b_ih, b_hh):
-            for row, vec in ((0, b_ih), (8, b_hh)):
+        def load_bias(d):
+            for row, vec in ((0, (b_ih_f, b_ih_b)[d]), (8, (b_hh_f, b_hh_b)[d])):
                 nc.sync.dma_start(out=bias_rows[row : row + 4, d, :], in_=vec.rearrange("(b u) -> b u", u=H))
 
         nc.vector.memset(zeros[:], 0.0)
@@ -91,22 +93,24 @@ def tile_predictionbilstm_kernel(
         make_identity(nc, ident[:])
         nc.scalar.activation(out=warm[:], in_=warm[:], func=ACT.Sigmoid)
 
-        load_x(nc.sync, 0, 1)
-        load_x(nc.sync, 1, 1)
-        load_w_scales(0, w_ih_f_scales)
-        load_x(nc.sync, 2, 2)
-        load_w_codes(0, w_ih_f_words)
-        load_bias(0, b_ih_f, b_hh_f)
-        load_x(nc.sync, 4, 2)
-        load_w_codes(1, w_ih_b_words)
-        load_w_scales(1, w_ih_b_scales)
-        load_bias(1, b_ih_b, b_hh_b)
-        load_x(nc.sync, 6, 2)
+        load_x(0, 1)
+        load_x(1, 1)
+        load_w_scales(0, (0, 1))
+        load_x(2, 2)
+        load_w_scales(0, (2, 3))
+        load_x(4, 1)
+        load_w_codes(0)
+        load_bias(0)
+        load_x(5, 1)
+        load_w_codes(1)
+        load_w_scales(1, range(4))
+        load_bias(1)
+        load_x(6, 2)
 
-        def make_bias_cols(d):
+        def make_bias_cols(d, copy):
             bias_ps = banks.tile([P, 32], F32, tag="bank")
             nc.tensor.matmul(out=bias_ps[:], lhsT=bias_rows[:, d, :], rhs=pick[:], start=True, stop=True)
-            nc.scalar.copy(out=bias_cols[:, d, :], in_=bias_ps[:])
+            copy(out=bias_cols[:, d, :], in_=bias_ps[:])
 
         busy_ps = banks.tile([P, P], F32, tag="bank")
 
@@ -122,28 +126,41 @@ def tile_predictionbilstm_kernel(
         x_scales = {}
         sums = {}
         sig_i, tanh_g, sig_o, cell, tanh_c, hidden = {}, {}, {}, {}, {}, {}
+        o_rows_ps, c_rows_ps, tanh_rows, out_ps = {}, {}, {}, {}
 
-        def flip_in(c, odd_copy):
+        def new_grouped(c):
             grouped[c] = quant.tile([P, PASSES, CHUNK, 4], BF16, align_bytes=64, name="grouped")
-            grouped_words = (
+
+        def grouped_words(c):
+            return (
                 grouped[c][:]
                 .rearrange("p g m t -> p (g m t)")
                 .bitcast(F32)
                 .rearrange("p (g m u) -> p g m u", g=PASSES, u=2)
             )
-            for j in range(CHUNK_TILES):
-                x_words = x_sb[:, c * CHUNK_TILES + j, :].bitcast(F32)
-                flipped = banks.tile([P, PASSES, 2, P], F32, tag="bank")
-                for g in range(PASSES):
-                    for u in range(2):
-                        nc.tensor.transpose(
-                            flipped[:, g, u, :], x_words[:, 256 * g + u : 256 * (g + 1) : 2], ident[:]
-                        )
-                copy = nc.vector.tensor_copy if j % 2 == 0 else odd_copy
-                copy(
-                    out=grouped_words[:, :, j * P : (j + 1) * P, :],
-                    in_=flipped[:].rearrange("p g u m -> p g m u"),
-                )
+
+        def transpose_words(out, c, j, g, u):
+            x_words = x_sb[:, c * CHUNK_TILES + j, :].bitcast(F32)
+            nc.tensor.transpose(out, x_words[:, 256 * g + u : 256 * (g + 1) : 2], ident[:])
+
+        def flip_in(c, j, copy):
+            flipped = banks.tile([P, PASSES, 2, P], F32, tag="bank")
+            for g in range(PASSES):
+                for u in range(2):
+                    transpose_words(flipped[:, g, u, :], c, j, g, u)
+            copy(
+                out=grouped_words(c)[:, :, j * P : (j + 1) * P, :],
+                in_=flipped[:].rearrange("p g u m -> p g m u"),
+            )
+
+        def flip_in_half(c, j, g, copy):
+            flipped = banks.tile([P, 2, P], F32, tag="bank")
+            for u in range(2):
+                transpose_words(flipped[:, u, :], c, j, g, u)
+            copy(
+                out=grouped_words(c)[:, g, j * P : (j + 1) * P, :],
+                in_=flipped[:].rearrange("p u m -> p m u"),
+            )
 
         def quantise(c):
             x_codes[c] = quant.tile([P, PASSES, CHUNK], U32, align_bytes=64, name="x_codes")
@@ -152,6 +169,17 @@ def tile_predictionbilstm_kernel(
                 out=x_codes[c][:].rearrange("p g m -> p (g m)").bitcast(FP8X4),
                 scales=x_scales[c][:].rearrange("p g m -> p (g m)"),
                 in_=grouped[c][:].rearrange("p g m t -> p (g m t)"),
+            )
+
+        def new_codes(c):
+            x_codes[c] = quant.tile([P, PASSES, CHUNK], U32, align_bytes=64, name="x_codes")
+            x_scales[c] = quant.tile([P, PASSES, CHUNK], U8, align_bytes=64, name="x_scales")
+
+        def quantise_pass(c, g):
+            nc.vector.quantize_mx(
+                out=x_codes[c][:, g, :].bitcast(FP8X4),
+                scales=x_scales[c][:, g, :],
+                in_=grouped[c][:, g, :, :].rearrange("p m t -> p (m t)"),
             )
 
         def gate_sums(c, d, block, acc):
@@ -173,23 +201,38 @@ def tile_predictionbilstm_kernel(
             gate_sums(c, d, GATE_I, acc[:, 0, :])
             gate_sums(c, d, GATE_G, acc[:, 1, :])
 
+        def multiply_gate(c, d, block):
+            acc = banks.tile([P, CHUNK], F32, tag="bank")
+            gate_sums(c, d, block, acc[:])
+
+        def multiply_gates(pairs, block):
+            acc = banks.tile([P, len(pairs), CHUNK], F32, tag="bank")
+            for s, (c, d) in enumerate(pairs):
+                gate_sums(c, d, block, acc[:, s, :])
+
         def multiply_out(c, dirs):
             acc = banks.tile([P, len(dirs), CHUNK], F32, tag="bank")
             for s, d in enumerate(dirs):
                 gate_sums(c, d, GATE_O, acc[:, s, :])
 
-        def new_chunk(c):
+        def new_chunk(c, names):
             for store, name in ((sig_i, "sig_i"), (tanh_g, "tanh_g"), (sig_o, "sig_o"), (cell, "cell"),
                                 (tanh_c, "tanh_c"), (hidden, "hidden")):
-                if c < CHUNKS - 1 or name != "hidden":
+                if name in names:
                     store[c] = work.tile([P, 2, CHUNK], F32, name=name)
 
         def part(tile_, dirs):
             return tile_[:, dirs[0] : dirs[-1] + 1, :]
 
-        def squash_in(c, d):
+        def squash_i(c, d):
             nc.scalar.activation(out=sig_i[c][:, d, :], in_=sums[c, d, GATE_I], func=ACT.Sigmoid, bias=bias_of(d, GATE_I))
+
+        def squash_g(c, d):
             nc.scalar.activation(out=tanh_g[c][:, d, :], in_=sums[c, d, GATE_G], func=ACT.Tanh, bias=bias_of(d, GATE_G))
+
+        def squash_in(c, d):
+            squash_i(c, d)
+            squash_g(c, d)
 
         def squash_out(c, d):
             nc.scalar.activation(out=sig_o[c][:, d, :], in_=sums[c, d, GATE_O], func=ACT.Sigmoid, bias=bias_of(d, GATE_O))
@@ -200,121 +243,138 @@ def tile_predictionbilstm_kernel(
         def squash_cell(c, dirs):
             nc.scalar.activation(out=part(tanh_c[c], dirs), in_=part(cell[c], dirs), func=ACT.Tanh)
 
-        def hidden_state(engine, c, dirs):
-            engine.tensor_mul(out=part(hidden[c], dirs), in0=part(sig_o[c], dirs), in1=part(tanh_c[c], dirs))
+        def hidden_state(c, dirs):
+            nc.vector.tensor_mul(out=part(hidden[c], dirs), in0=part(sig_o[c], dirs), in1=part(tanh_c[c], dirs))
 
-        flipped_back = {}
-
-        def flip_out(c, dirs):
-            flipped_back[c, dirs] = banks.tile([P, CHUNK_TILES, len(dirs), H], F32, tag="bank", name="flipped_back")
+        def flip(source, c, dirs):
+            rows_ps = banks.tile([P, CHUNK_TILES, len(dirs), H], F32, tag="bank")
             for j in range(CHUNK_TILES):
                 for s, d in enumerate(dirs):
-                    nc.tensor.transpose(flipped_back[c, dirs][:, j, s, :], hidden[c][:, d, j * P : (j + 1) * P], ident[:])
+                    nc.tensor.transpose(rows_ps[:, j, s, :], source[c][:, d, j * P : (j + 1) * P], ident[:])
+            return rows_ps
+
+        def flip_hidden(c, dirs):
+            out_ps[c, dirs] = flip(hidden, c, dirs)
+
+        def send(h_rows, c, dirs):
+            tiles = slice(c * CHUNK_TILES, (c + 1) * CHUNK_TILES)
+            nc.sync.dma_start(
+                out=out_rows[:, tiles, dirs[0] * H : (dirs[-1] + 1) * H],
+                in_=h_rows[:].rearrange("p j d u -> p j (d u)"),
+            )
 
         def store(copy, c, dirs):
-            h_rows = outbound.tile([P, CHUNK_TILES, len(dirs) * H], F32, name="h_rows")
-            copy(out=h_rows[:], in_=flipped_back[c, dirs][:].rearrange("p j d u -> p j (d u)"))
-            tiles = slice(c * CHUNK_TILES, (c + 1) * CHUNK_TILES)
-            nc.sync.dma_start(out=out_rows[:, tiles, dirs[0] * H : (dirs[-1] + 1) * H], in_=h_rows[:])
+            h_rows = outbound.tile([P, CHUNK_TILES, len(dirs), H], F32, name="h_rows")
+            copy(out=h_rows[:], in_=out_ps[c, dirs][:])
+            send(h_rows, c, dirs)
 
-        gate_rows, cell_rows_ps = {}, {}
+        def flip_gate(c, dirs):
+            o_rows_ps[c, dirs] = flip(sig_o, c, dirs)
 
-        def flip_part(source, c, d):
-            flipped_part = banks.tile([P, CHUNK_TILES, H], F32, tag="bank")
-            for j in range(CHUNK_TILES):
-                nc.tensor.transpose(flipped_part[:, j, :], source[c][:, d, j * P : (j + 1) * P], ident[:])
-            return flipped_part
+        def flip_cell(c, dirs):
+            c_rows_ps[c, dirs] = flip(cell, c, dirs)
 
-        def flip_gate(c, d):
-            gate_ps = flip_part(sig_o, c, d)
-            gate_rows[c, d] = outbound.tile([P, CHUNK_TILES, H], F32, name="gate_rows")
-            nc.vector.tensor_copy(out=gate_rows[c, d][:], in_=gate_ps[:])
+        def squash_cell_rows(c, dirs):
+            tanh_rows[c, dirs] = outbound.tile([P, CHUNK_TILES, len(dirs), H], F32, name="tanh_rows")
+            nc.scalar.activation(out=tanh_rows[c, dirs][:], in_=c_rows_ps[c, dirs][:], func=ACT.Tanh)
 
-        def finish(c, d):
-            h_rows = outbound.tile([P, CHUNK_TILES, H], F32, name="h_rows")
-            nc.vector.tensor_mul(out=h_rows[:], in0=cell_rows_ps[c, d][:], in1=gate_rows[c, d][:])
-            tiles = slice(c * CHUNK_TILES, (c + 1) * CHUNK_TILES)
-            nc.sync.dma_start(out=out_rows[:, tiles, d * H : (d + 1) * H], in_=h_rows[:])
+        def finish(c, dirs):
+            h_rows = outbound.tile([P, CHUNK_TILES, len(dirs), H], F32, name="h_rows")
+            nc.vector.tensor_mul(out=h_rows[:], in0=o_rows_ps[c, dirs][:], in1=tanh_rows[c, dirs][:])
+            send(h_rows, c, dirs)
 
         nc.vector.tensor_add(out=pick[:], in0=ident[:, 0:32], in1=ident[:, 8:40])
         FWD, BWD = 0, 1
         by_vector, by_scalar = nc.vector.tensor_copy, nc.scalar.copy
+        IN = ("sig_i", "tanh_g", "sig_o", "cell")
+        ALL = IN + ("tanh_c", "hidden")
 
-        def multiply(c, d):
-            multiply_in(c, d)
-            multiply_out(c, (d,))
-
-        new_chunk(0)
-        new_chunk(1)
-        keep_busy(4)
-        flip_in(0, by_scalar)
+        new_chunk(0, ALL)
+        new_chunk(1, ALL)
+        keep_busy(15)
+        new_grouped(0)
+        flip_in_half(0, 0, 0, by_vector)
+        flip_in_half(0, 1, 0, by_scalar)
+        flip_in_half(0, 0, 1, by_vector)
+        flip_in_half(0, 1, 1, by_scalar)
         quantise(0)
         keep_busy(2)
-        flip_in(1, by_scalar)
+        new_grouped(1)
+        flip_in(1, 0, by_scalar)
+        flip_in_half(1, 1, 0, by_scalar)
+        flip_in_half(1, 1, 1, by_vector)
         quantise(1)
-        make_bias_cols(FWD)
-        multiply(0, FWD)
+        new_grouped(2)
+        flip_in(2, 0, by_vector)
+        keep_busy(3)
+        make_bias_cols(FWD, by_scalar)
+        multiply_gate(0, FWD, GATE_I)
+        multiply_gate(0, FWD, GATE_G)
+        multiply_gates(((0, FWD),), GATE_O)
         squash_in(0, FWD)
         squash_out(0, FWD)
         cell_state(0, (FWD,))
-        flip_in(2, by_vector)
-        squash_cell(0, (FWD,))
-        multiply(1, FWD)
+        multiply_in(1, FWD)
+        multiply_gates(((1, FWD),), GATE_O)
         squash_in(1, FWD)
+        squash_cell(0, (FWD,))
         squash_out(1, FWD)
         cell_state(1, (FWD,))
-        hidden_state(nc.vector, 0, (FWD,))
+        flip_in(2, 1, by_vector)
         quantise(2)
-        multiply_in(0, BWD)
-        make_bias_cols(BWD)
-        multiply_out(0, (BWD,))
+        make_bias_cols(BWD, by_scalar)
         squash_cell(1, (FWD,))
-        hidden_state(nc.vector, 1, (FWD,))
-        multiply(1, BWD)
+        multiply_in(0, BWD)
+        multiply_gates(((0, BWD),), GATE_O)
         squash_in(0, BWD)
-        cell_state(0, (BWD,))
-        squash_in(1, BWD)
-        flip_in(3, by_vector)
+        multiply_in(1, BWD)
+        multiply_gates(((1, BWD),), GATE_O)
         squash_out(0, BWD)
+        squash_in(1, BWD)
+        cell_state(0, (BWD,))
+        squash_out(1, BWD)
         squash_cell(0, (BWD,))
-        hidden_state(nc.vector, 0, (BWD,))
+        new_grouped(3)
+        flip_in(3, 0, by_vector)
         cell_state(1, (BWD,))
+        flip_in(3, 1, by_vector)
         quantise(3)
-        new_chunk(2)
+        hidden_state(0, BOTH)
+        new_chunk(2, IN)
         for d in BOTH:
             multiply_in(2, d)
         multiply_out(2, BOTH)
-        for d in BOTH:
-            squash_in(2, d)
-        squash_out(1, BWD)
         squash_cell(1, (BWD,))
+        squash_in(2, FWD)
+        squash_in(2, BWD)
         cell_state(2, BOTH)
-        for d in BOTH:
-            squash_out(2, d)
-        squash_cell(2, BOTH)
-        flip_out(0, BOTH)
-        store(by_vector, 0, BOTH)
-        hidden_state(nc.vector, 1, (BWD,))
-        hidden_state(nc.vector, 2, BOTH)
-        new_chunk(3)
+        hidden_state(1, BOTH)
+        new_chunk(3, IN)
         for d in BOTH:
             multiply_in(3, d)
         for d in BOTH:
-            multiply_out(3, (d,))
-        flip_out(1, BOTH)
-        flip_out(2, BOTH)
+            squash_out(2, d)
+        flip_hidden(0, BOTH)
+        flip_cell(2, BOTH)
         for d in BOTH:
-            squash_in(3, d)
-            cell_state(3, (d,))
+            multiply_out(3, (d,))
+        flip_hidden(1, BOTH)
+        flip_gate(2, BOTH)
+        squash_in(3, FWD)
+        cell_state(3, (FWD,))
+        store(by_vector, 0, BOTH)
+        squash_in(3, BWD)
+        cell_state(3, (BWD,))
+        squash_cell_rows(2, BOTH)
         store(by_vector, 1, BOTH)
+        for d in BOTH:
+            flip_cell(3, (d,))
+        finish(2, BOTH)
         for d in BOTH:
             squash_out(3, d)
         for d in BOTH:
-            flip_gate(3, d)
+            squash_cell_rows(3, (d,))
         for d in BOTH:
-            squash_cell(3, (d,))
-        store(by_scalar, 2, BOTH)
+            flip_gate(3, (d,))
         for d in BOTH:
-            cell_rows_ps[3, d] = flip_part(tanh_c, 3, d)
-        for d in BOTH:
-            finish(3, d)
+            finish(3, (d,))

@@ -95,19 +95,17 @@ def tile_predictionbilstm_kernel(
 
         load_x(0, 1)
         load_x(1, 1)
-        load_w_scales(0, (0, 1))
+        load_w_scales(0, range(4))
         load_x(2, 2)
-        load_w_scales(0, (2, 3))
-        load_x(4, 1)
         load_w_codes(0)
         load_bias(0)
-        load_x(5, 1)
+        load_x(4, 2)
         load_w_codes(1)
         load_w_scales(1, range(4))
         load_bias(1)
         load_x(6, 2)
 
-        def make_bias_cols(d, copy):
+        def make_bias_cols(d, copy=nc.scalar.copy):
             bias_ps = banks.tile([P, 32], F32, tag="bank")
             nc.tensor.matmul(out=bias_ps[:], lhsT=bias_rows[:, d, :], rhs=pick[:], start=True, stop=True)
             copy(out=bias_cols[:, d, :], in_=bias_ps[:])
@@ -291,87 +289,83 @@ def tile_predictionbilstm_kernel(
 
         new_chunk(0, ALL)
         new_chunk(1, ALL)
-        keep_busy(15)
+        keep_busy(18)
         new_grouped(0)
         flip_in_half(0, 0, 0, by_vector)
-        flip_in_half(0, 1, 0, by_scalar)
-        flip_in_half(0, 0, 1, by_vector)
+        flip_in_half(0, 0, 1, by_scalar)
+        flip_in_half(0, 1, 0, by_vector)
         flip_in_half(0, 1, 1, by_scalar)
         quantise(0)
-        keep_busy(2)
+        keep_busy(9)
         new_grouped(1)
         flip_in(1, 0, by_scalar)
-        flip_in_half(1, 1, 0, by_scalar)
-        flip_in_half(1, 1, 1, by_vector)
+        flip_in(1, 1, by_vector)
         quantise(1)
-        new_grouped(2)
-        flip_in(2, 0, by_vector)
-        keep_busy(3)
-        make_bias_cols(FWD, by_scalar)
-        multiply_gate(0, FWD, GATE_I)
-        multiply_gate(0, FWD, GATE_G)
+        multiply_in(0, FWD)
+        make_bias_cols(FWD)
         multiply_gates(((0, FWD),), GATE_O)
         squash_in(0, FWD)
         squash_out(0, FWD)
+        new_grouped(2)
+        flip_in(2, 0, by_vector)
         cell_state(0, (FWD,))
-        multiply_in(1, FWD)
-        multiply_gates(((1, FWD),), GATE_O)
-        squash_in(1, FWD)
-        squash_cell(0, (FWD,))
-        squash_out(1, FWD)
-        cell_state(1, (FWD,))
         flip_in(2, 1, by_vector)
         quantise(2)
-        make_bias_cols(BWD, by_scalar)
-        squash_cell(1, (FWD,))
+        squash_cell(0, (FWD,))
+        multiply_in(1, FWD)
+        make_bias_cols(BWD)
         multiply_in(0, BWD)
-        multiply_gates(((0, BWD),), GATE_O)
+        multiply_gates(((1, FWD),), GATE_O)
+        squash_in(1, FWD)
         squash_in(0, BWD)
+        cell_state(1, (FWD,))
         multiply_in(1, BWD)
-        multiply_gates(((1, BWD),), GATE_O)
-        squash_out(0, BWD)
-        squash_in(1, BWD)
+        squash_out(1, FWD)
+        squash_cell(1, (FWD,))
         cell_state(0, (BWD,))
-        squash_out(1, BWD)
-        squash_cell(0, (BWD,))
+        squash_in(1, BWD)
+        multiply_gates(((0, BWD), (1, BWD)), GATE_O)
         new_grouped(3)
         flip_in(3, 0, by_vector)
-        cell_state(1, (BWD,))
         flip_in(3, 1, by_vector)
+        squash_cell(0, (BWD,))
+        squash_out(0, BWD)
+        squash_out(1, BWD)
         quantise(3)
+        cell_state(1, (BWD,))
         hidden_state(0, BOTH)
         new_chunk(2, IN)
         for d in BOTH:
             multiply_in(2, d)
         multiply_out(2, BOTH)
+        for d in BOTH:
+            squash_in(2, d)
         squash_cell(1, (BWD,))
-        squash_in(2, FWD)
-        squash_in(2, BWD)
         cell_state(2, BOTH)
         hidden_state(1, BOTH)
         new_chunk(3, IN)
         for d in BOTH:
             multiply_in(3, d)
-        for d in BOTH:
-            squash_out(2, d)
-        flip_hidden(0, BOTH)
-        flip_cell(2, BOTH)
+        squash_out(2, FWD)
         for d in BOTH:
             multiply_out(3, (d,))
+        flip_hidden(0, BOTH)
+        flip_cell(2, BOTH)
         flip_hidden(1, BOTH)
-        flip_gate(2, BOTH)
         squash_in(3, FWD)
+        squash_out(2, BWD)
+        squash_in(3, BWD)
         cell_state(3, (FWD,))
         store(by_vector, 0, BOTH)
-        squash_in(3, BWD)
         cell_state(3, (BWD,))
         squash_cell_rows(2, BOTH)
-        store(by_vector, 1, BOTH)
+        flip_gate(2, BOTH)
         for d in BOTH:
             flip_cell(3, (d,))
-        finish(2, BOTH)
+        store(by_vector, 1, BOTH)
         for d in BOTH:
             squash_out(3, d)
+        finish(2, BOTH)
         for d in BOTH:
             squash_cell_rows(3, (d,))
         for d in BOTH:

@@ -298,25 +298,26 @@ def tile_predictionbilstm_kernel(
         quantise(0)
         keep_busy(9)
         new_grouped(1)
-        flip_in(1, 0, by_scalar)
-        flip_in(1, 1, by_vector)
+        flip_in(1, 0, by_vector)
+        flip_in(1, 1, by_scalar)
         quantise(1)
         multiply_in(0, FWD)
         make_bias_cols(FWD)
         multiply_gates(((0, FWD),), GATE_O)
+        keep_busy(4)
         squash_in(0, FWD)
         squash_out(0, FWD)
         new_grouped(2)
         flip_in(2, 0, by_vector)
-        cell_state(0, (FWD,))
         flip_in(2, 1, by_vector)
+        cell_state(0, (FWD,))
         quantise(2)
-        squash_cell(0, (FWD,))
         multiply_in(1, FWD)
         make_bias_cols(BWD)
         multiply_in(0, BWD)
         multiply_gates(((1, FWD),), GATE_O)
         squash_in(1, FWD)
+        squash_cell(0, (FWD,))
         squash_in(0, BWD)
         cell_state(1, (FWD,))
         multiply_in(1, BWD)
@@ -331,8 +332,8 @@ def tile_predictionbilstm_kernel(
         squash_cell(0, (BWD,))
         squash_out(0, BWD)
         squash_out(1, BWD)
-        quantise(3)
         cell_state(1, (BWD,))
+        quantise(3)
         hidden_state(0, BOTH)
         new_chunk(2, IN)
         for d in BOTH:
@@ -347,16 +348,16 @@ def tile_predictionbilstm_kernel(
         for d in BOTH:
             multiply_in(3, d)
         squash_out(2, FWD)
-        for d in BOTH:
-            multiply_out(3, (d,))
         flip_hidden(0, BOTH)
         flip_cell(2, BOTH)
         flip_hidden(1, BOTH)
+        for d in BOTH:
+            multiply_out(3, (d,))
         squash_in(3, FWD)
         squash_out(2, BWD)
         squash_in(3, BWD)
-        cell_state(3, (FWD,))
         store(by_vector, 0, BOTH)
+        cell_state(3, (FWD,))
         cell_state(3, (BWD,))
         squash_cell_rows(2, BOTH)
         flip_gate(2, BOTH)

@@ -62,7 +62,7 @@ def tile_predictionbilstm_kernel(
         pick = keep.tile([P, 32], BF16)
         bias_cols = keep.tile([P, 2, 32], F32)
         warm = keep.tile([P, 1], F32)
-        zeros = keep.tile([P, P], BF16)
+        zeros = keep.tile([P, P], F32)
 
         def load_x(first, count):
             nc.sync.dma_start(out=x_sb[:, first : first + count, :], in_=x_rows[:, first : first + count, :])
@@ -289,14 +289,14 @@ def tile_predictionbilstm_kernel(
 
         new_chunk(0, ALL)
         new_chunk(1, ALL)
-        keep_busy(18)
+        keep_busy(4)
         new_grouped(0)
         flip_in_half(0, 0, 0, by_vector)
         flip_in_half(0, 0, 1, by_scalar)
         flip_in_half(0, 1, 0, by_vector)
         flip_in_half(0, 1, 1, by_scalar)
         quantise(0)
-        keep_busy(9)
+        keep_busy(2)
         new_grouped(1)
         flip_in(1, 0, by_vector)
         flip_in(1, 1, by_scalar)
@@ -304,7 +304,7 @@ def tile_predictionbilstm_kernel(
         multiply_in(0, FWD)
         make_bias_cols(FWD)
         multiply_gates(((0, FWD),), GATE_O)
-        keep_busy(4)
+        keep_busy(1)
         squash_in(0, FWD)
         squash_out(0, FWD)
         new_grouped(2)

@@ -100,9 +100,9 @@ def tile_predictionbilstm_kernel(
         load_w_codes(0)
         load_bias(0)
         load_x(4, 2)
+        load_bias(1)
         load_w_codes(1)
         load_w_scales(1, range(4))
-        load_bias(1)
         load_x(6, 2)
 
         def make_bias_cols(d, copy=nc.scalar.copy):
@@ -313,11 +313,11 @@ def tile_predictionbilstm_kernel(
         cell_state(0, (FWD,))
         quantise(2)
         multiply_in(1, FWD)
-        make_bias_cols(BWD)
         multiply_in(0, BWD)
         multiply_gates(((1, FWD),), GATE_O)
         squash_in(1, FWD)
         squash_cell(0, (FWD,))
+        make_bias_cols(BWD)
         squash_in(0, BWD)
         cell_state(1, (FWD,))
         multiply_in(1, BWD)

@@ -100,9 +100,9 @@ def tile_predictionbilstm_kernel(
         load_w_codes(0)
         load_bias(0)
         load_x(4, 2)
-        load_bias(1)
-        load_w_codes(1)
         load_w_scales(1, range(4))
+        load_w_codes(1)
+        load_bias(1)
         load_x(6, 2)
 
         def make_bias_cols(d, copy=nc.scalar.copy):

from contextlib import ExitStack

import concourse.mybir as mybir
from concourse.masks import make_identity

F32 = mybir.dt.float32
BF16 = mybir.dt.bfloat16
I32 = mybir.dt.int32
U32 = mybir.dt.uint32
U8 = mybir.dt.uint8
FP8X4 = mybir.dt.float8_e4m3fn_x4
ACT = mybir.ActivationFunctionType

P = 128
ROWS = 1024
K = 1024
H = 128
PASSES = K // (4 * P)
ROW_TILES = ROWS // P
CHUNK_TILES = 2
CHUNK = CHUNK_TILES * P
CHUNKS = ROW_TILES // CHUNK_TILES
GATE_I, GATE_G, GATE_O = 0, 2, 3

FLOPS = 2 * ROWS * K * 2 * 3 * H
BYTES = ROWS * K * 2 + 2 * (K * 3 * H + (K // 32) * 3 * H + 2 * 3 * H * 2) + ROWS * 2 * H * 4


def tile_predictionbilstm_kernel(
    tc,
    V_cells,
    w_ih_f_words,
    w_ih_f_scales,
    w_hh_f,
    b_ih_f,
    b_hh_f,
    w_ih_b_words,
    w_ih_b_scales,
    w_hh_b,
    b_ih_b,
    b_hh_b,
    out,
):
    nc = tc.nc
    x_rows = V_cells.rearrange("(p t) k -> p t k", t=ROW_TILES)
    out_rows = out.rearrange("(p t) c -> p t c", t=ROW_TILES)
    BOTH = (0, 1)

    with ExitStack() as ctx:
        keep = ctx.enter_context(tc.tile_pool(name="keep", bufs=1))
        quant = ctx.enter_context(tc.tile_pool(name="quant", bufs=CHUNKS))
        work = ctx.enter_context(tc.tile_pool(name="work", bufs=3))
        outbound = ctx.enter_context(tc.tile_pool(name="outbound", bufs=CHUNKS + 1))
        banks = ctx.enter_context(tc.psum_pool(name="banks", bufs=8))
        ctx.enter_context(tc.manual_schedule())

        x_sb = keep.tile([P, ROW_TILES, K], BF16)
        w_codes = keep.tile([P, 2, PASSES, 4 * H], U32, align_bytes=64)
        w_scales = keep.tile([P, 2, PASSES, 4 * H], U8, align_bytes=64)
        bias_rows = keep.tile([P, 2, H], BF16)
        ident = keep.tile([P, P], F32)
        pick = keep.tile([P, 32], BF16)
        bias_cols = keep.tile([P, 2, 32], F32)
        warm = keep.tile([P, 1], F32)
        zeros = keep.tile([P, P], F32)

        def load_x(first, count):
            nc.sync.dma_start(out=x_sb[:, first : first + count, :], in_=x_rows[:, first : first + count, :])

        def load_w_codes(d):
            words = (w_ih_f_words, w_ih_b_words)[d]
            nc.sync.dma_start(
                out=w_codes[:, d, :, :].bitcast(I32),
                in_=words.rearrange("g p n t -> p g (n t)").bitcast(I32),
            )

        def load_w_scales(d, quads):
            scales = (w_ih_f_scales, w_ih_b_scales)[d]
            for quad in quads:
                nc.sync.dma_start(
                    out=w_scales[32 * quad : 32 * quad + 4, d, :, :].bitcast(I32),
                    in_=scales[:, 4 * quad : 4 * quad + 4, :].rearrange("g r n -> r g n").bitcast(I32),
                )

        def load_bias(d):
            for row, vec in ((0, (b_ih_f, b_ih_b)[d]), (8, (b_hh_f, b_hh_b)[d])):
                nc.sync.dma_start(out=bias_rows[row : row + 4, d, :], in_=vec.rearrange("(b u) -> b u", u=H))

        nc.vector.memset(zeros[:], 0.0)
        nc.vector.memset(w_scales[:].rearrange("p d g n -> p (d g n)").bitcast(I32), 0)
        nc.vector.memset(bias_rows[:].rearrange("p d u -> p (d u)"), 0.0)
        nc.vector.memset(warm[:], 0.0)
        make_identity(nc, ident[:])
        nc.scalar.activation(out=warm[:], in_=warm[:], func=ACT.Sigmoid)

        load_x(0, 1)
        load_x(1, 1)
        load_w_scales(0, range(4))
        load_x(2, 2)
        load_w_codes(0)
        load_bias(0)
        load_x(4, 2)
        load_w_scales(1, range(4))
        load_w_codes(1)
        load_bias(1)
        load_x(6, 2)

        def make_bias_cols(d, copy=nc.scalar.copy):
            bias_ps = banks.tile([P, 32], F32, tag="bank")
            nc.tensor.matmul(out=bias_ps[:], lhsT=bias_rows[:, d, :], rhs=pick[:], start=True, stop=True)
            copy(out=bias_cols[:, d, :], in_=bias_ps[:])

        busy_ps = banks.tile([P, P], F32, tag="bank")

        def keep_busy(times):
            for repeat in range(times):
                nc.tensor.matmul(out=busy_ps[:], lhsT=zeros[:], rhs=zeros[:], start=True, stop=True)

        def bias_of(d, block):
            return bias_cols[:, d, block : block + 1]

        grouped = {}
        x_codes = {}
        x_scales = {}
        sums = {}
        sig_i, tanh_g, sig_o, cell, tanh_c, hidden = {}, {}, {}, {}, {}, {}
        o_rows_ps, c_rows_ps, tanh_rows, out_ps = {}, {}, {}, {}

        def new_grouped(c):
            grouped[c] = quant.tile([P, PASSES, CHUNK, 4], BF16, align_bytes=64, name="grouped")

        def grouped_words(c):
            return (
                grouped[c][:]
                .rearrange("p g m t -> p (g m t)")
                .bitcast(F32)
                .rearrange("p (g m u) -> p g m u", g=PASSES, u=2)
            )

        def transpose_words(out, c, j, g, u):
            x_words = x_sb[:, c * CHUNK_TILES + j, :].bitcast(F32)
            nc.tensor.transpose(out, x_words[:, 256 * g + u : 256 * (g + 1) : 2], ident[:])

        def flip_in(c, j, copy):
            flipped = banks.tile([P, PASSES, 2, P], F32, tag="bank")
            for g in range(PASSES):
                for u in range(2):
                    transpose_words(flipped[:, g, u, :], c, j, g, u)
            copy(
                out=grouped_words(c)[:, :, j * P : (j + 1) * P, :],
                in_=flipped[:].rearrange("p g u m -> p g m u"),
            )

        def flip_in_half(c, j, g, copy):
            flipped = banks.tile([P, 2, P], F32, tag="bank")
            for u in range(2):
                transpose_words(flipped[:, u, :], c, j, g, u)
            copy(
                out=grouped_words(c)[:, g, j * P : (j + 1) * P, :],
                in_=flipped[:].rearrange("p u m -> p m u"),
            )

        def quantise(c):
            x_codes[c] = quant.tile([P, PASSES, CHUNK], U32, align_bytes=64, name="x_codes")
            x_scales[c] = quant.tile([P, PASSES, CHUNK], U8, align_bytes=64, name="x_scales")
            nc.vector.quantize_mx(
                out=x_codes[c][:].rearrange("p g m -> p (g m)").bitcast(FP8X4),
                scales=x_scales[c][:].rearrange("p g m -> p (g m)"),
                in_=grouped[c][:].rearrange("p g m t -> p (g m t)"),
            )

        def new_codes(c):
            x_codes[c] = quant.tile([P, PASSES, CHUNK], U32, align_bytes=64, name="x_codes")
            x_scales[c] = quant.tile([P, PASSES, CHUNK], U8, align_bytes=64, name="x_scales")

        def quantise_pass(c, g):
            nc.vector.quantize_mx(
                out=x_codes[c][:, g, :].bitcast(FP8X4),
                scales=x_scales[c][:, g, :],
                in_=grouped[c][:, g, :, :].rearrange("p m t -> p (m t)"),
            )

        def gate_sums(c, d, block, acc):
            sums[c, d, block] = acc
            units = slice(block * H, (block + 1) * H)
            for g in range(PASSES):
                nc.tensor.matmul_mx(
                    out=acc,
                    lhsT=w_codes[:, d, g, units].bitcast(FP8X4),
                    lhsT_scale=w_scales[:, d, g, units],
                    rhs=x_codes[c][:, g, :].bitcast(FP8X4),
                    rhs_scale=x_scales[c][:, g, :],
                    start=(g == 0),
                    stop=(g == PASSES - 1),
                )

        def multiply_in(c, d):
            acc = banks.tile([P, 2, CHUNK], F32, tag="bank")
            gate_sums(c, d, GATE_I, acc[:, 0, :])
            gate_sums(c, d, GATE_G, acc[:, 1, :])

        def multiply_gate(c, d, block):
            acc = banks.tile([P, CHUNK], F32, tag="bank")
            gate_sums(c, d, block, acc[:])

        def multiply_gates(pairs, block):
            acc = banks.tile([P, len(pairs), CHUNK], F32, tag="bank")
            for s, (c, d) in enumerate(pairs):
                gate_sums(c, d, block, acc[:, s, :])

        def multiply_out(c, dirs):
            acc = banks.tile([P, len(dirs), CHUNK], F32, tag="bank")
            for s, d in enumerate(dirs):
                gate_sums(c, d, GATE_O, acc[:, s, :])

        def new_chunk(c, names):
            for store, name in ((sig_i, "sig_i"), (tanh_g, "tanh_g"), (sig_o, "sig_o"), (cell, "cell"),
                                (tanh_c, "tanh_c"), (hidden, "hidden")):
                if name in names:
                    store[c] = work.tile([P, 2, CHUNK], F32, name=name)

        def part(tile_, dirs):
            return tile_[:, dirs[0] : dirs[-1] + 1, :]

        def squash_i(c, d):
            nc.scalar.activation(out=sig_i[c][:, d, :], in_=sums[c, d, GATE_I], func=ACT.Sigmoid, bias=bias_of(d, GATE_I))

        def squash_g(c, d):
            nc.scalar.activation(out=tanh_g[c][:, d, :], in_=sums[c, d, GATE_G], func=ACT.Tanh, bias=bias_of(d, GATE_G))

        def squash_in(c, d):
            squash_i(c, d)
            squash_g(c, d)

        def squash_out(c, d):
            nc.scalar.activation(out=sig_o[c][:, d, :], in_=sums[c, d, GATE_O], func=ACT.Sigmoid, bias=bias_of(d, GATE_O))

        def cell_state(c, dirs):
            nc.vector.tensor_mul(out=part(cell[c], dirs), in0=part(sig_i[c], dirs), in1=part(tanh_g[c], dirs))

        def squash_cell(c, dirs):
            nc.scalar.activation(out=part(tanh_c[c], dirs), in_=part(cell[c], dirs), func=ACT.Tanh)

        def hidden_state(c, dirs):
            nc.vector.tensor_mul(out=part(hidden[c], dirs), in0=part(sig_o[c], dirs), in1=part(tanh_c[c], dirs))

        def flip(source, c, dirs):
            rows_ps = banks.tile([P, CHUNK_TILES, len(dirs), H], F32, tag="bank")
            for j in range(CHUNK_TILES):
                for s, d in enumerate(dirs):
                    nc.tensor.transpose(rows_ps[:, j, s, :], source[c][:, d, j * P : (j + 1) * P], ident[:])
            return rows_ps

        def flip_hidden(c, dirs):
            out_ps[c, dirs] = flip(hidden, c, dirs)

        def send(h_rows, c, dirs):
            tiles = slice(c * CHUNK_TILES, (c + 1) * CHUNK_TILES)
            nc.sync.dma_start(
                out=out_rows[:, tiles, dirs[0] * H : (dirs[-1] + 1) * H],
                in_=h_rows[:].rearrange("p j d u -> p j (d u)"),
            )

        def store(copy, c, dirs):
            h_rows = outbound.tile([P, CHUNK_TILES, len(dirs), H], F32, name="h_rows")
            copy(out=h_rows[:], in_=out_ps[c, dirs][:])
            send(h_rows, c, dirs)

        def flip_gate(c, dirs):
            o_rows_ps[c, dirs] = flip(sig_o, c, dirs)

        def flip_cell(c, dirs):
            c_rows_ps[c, dirs] = flip(cell, c, dirs)

        def squash_cell_rows(c, dirs):
            tanh_rows[c, dirs] = outbound.tile([P, CHUNK_TILES, len(dirs), H], F32, name="tanh_rows")
            nc.scalar.activation(out=tanh_rows[c, dirs][:], in_=c_rows_ps[c, dirs][:], func=ACT.Tanh)

        def finish(c, dirs):
            h_rows = outbound.tile([P, CHUNK_TILES, len(dirs), H], F32, name="h_rows")
            nc.vector.tensor_mul(out=h_rows[:], in0=o_rows_ps[c, dirs][:], in1=tanh_rows[c, dirs][:])
            send(h_rows, c, dirs)

        nc.vector.tensor_add(out=pick[:], in0=ident[:, 0:32], in1=ident[:, 8:40])
        FWD, BWD = 0, 1
        by_vector, by_scalar = nc.vector.tensor_copy, nc.scalar.copy
        IN = ("sig_i", "tanh_g", "sig_o", "cell")
        ALL = IN + ("tanh_c", "hidden")

        new_chunk(0, ALL)
        new_chunk(1, ALL)
        keep_busy(4)
        new_grouped(0)
        flip_in_half(0, 0, 0, by_vector)
        flip_in_half(0, 0, 1, by_scalar)
        flip_in_half(0, 1, 0, by_vector)
        flip_in_half(0, 1, 1, by_scalar)
        quantise(0)
        keep_busy(2)
        new_grouped(1)
        flip_in(1, 0, by_vector)
        flip_in(1, 1, by_scalar)
        quantise(1)
        multiply_in(0, FWD)
        make_bias_cols(FWD)
        multiply_gates(((0, FWD),), GATE_O)
        keep_busy(1)
        squash_in(0, FWD)
        squash_out(0, FWD)
        new_grouped(2)
        flip_in(2, 0, by_vector)
        flip_in(2, 1, by_vector)
        cell_state(0, (FWD,))
        quantise(2)
        multiply_in(1, FWD)
        multiply_in(0, BWD)
        multiply_gates(((1, FWD),), GATE_O)
        squash_in(1, FWD)
        squash_cell(0, (FWD,))
        make_bias_cols(BWD)
        squash_in(0, BWD)
        cell_state(1, (FWD,))
        multiply_in(1, BWD)
        squash_out(1, FWD)
        squash_cell(1, (FWD,))
        cell_state(0, (BWD,))
        squash_in(1, BWD)
        multiply_gates(((0, BWD), (1, BWD)), GATE_O)
        new_grouped(3)
        flip_in(3, 0, by_vector)
        flip_in(3, 1, by_vector)
        squash_cell(0, (BWD,))
        squash_out(0, BWD)
        squash_out(1, BWD)
        cell_state(1, (BWD,))
        quantise(3)
        hidden_state(0, BOTH)
        new_chunk(2, IN)
        for d in BOTH:
            multiply_in(2, d)
        multiply_out(2, BOTH)
        for d in BOTH:
            squash_in(2, d)
        squash_cell(1, (BWD,))
        cell_state(2, BOTH)
        hidden_state(1, BOTH)
        new_chunk(3, IN)
        for d in BOTH:
            multiply_in(3, d)
        squash_out(2, FWD)
        flip_hidden(0, BOTH)
        flip_cell(2, BOTH)
        flip_hidden(1, BOTH)
        for d in BOTH:
            multiply_out(3, (d,))
        squash_in(3, FWD)
        squash_out(2, BWD)
        squash_in(3, BWD)
        store(by_vector, 0, BOTH)
        cell_state(3, (FWD,))
        cell_state(3, (BWD,))
        squash_cell_rows(2, BOTH)
        flip_gate(2, BOTH)
        for d in BOTH:
            flip_cell(3, (d,))
        store(by_vector, 1, BOTH)
        for d in BOTH:
            squash_out(3, d)
        finish(2, BOTH)
        for d in BOTH:
            squash_cell_rows(3, (d,))
        for d in BOTH:
            flip_gate(3, (d,))
        for d in BOTH:
            finish(3, (d,))
